import numpy as np
import ml_dtypes


def mxq(x, axis, fmt="e4m3"):
    dtype, down = {"e4m3": (ml_dtypes.float8_e4m3fn, 7), "e5m2": (ml_dtypes.float8_e5m2, 14)}[fmt]
    v = np.moveaxis(np.asarray(x, np.float32).astype(ml_dtypes.bfloat16).astype(np.float64), axis, -1)
    blocks = v.reshape(v.shape[:-1] + (-1, 32))
    amax = np.abs(blocks).max(-1, keepdims=True)
    byte = np.maximum(np.where(amax > 0, np.frexp(amax)[1] - 1 + 127, 0) - down, 1)
    scale = np.exp2(byte - 127.0)
    codes = (blocks / scale).astype(np.float32).astype(dtype).astype(np.float64)
    return np.moveaxis((codes * scale).reshape(v.shape), -1, axis)


WIDE = False


def mx_kscale(k):
    if not WIDE:
        return np.ones(k)
    levels = np.array([10, -10, 5, -5, 0])
    a = np.random.permutation(np.resize(levels, k // 512 * 4)).reshape(k // 512, 4)
    idx = np.arange(k)
    return np.exp2(a[idx // 512, idx % 128 // 32])


BF16 = ml_dtypes.bfloat16


def bf(x):
    return np.asarray(x, np.float32).astype(BF16)


def f64(x):
    return np.asarray(x).astype(np.float64)


E2M1 = np.array([0.0, 0.5, 1.0, 1.5, 2.0, 3.0, 4.0, 6.0, -0.0, -0.5, -1.0, -1.5, -2.0, -3.0, -4.0, -6.0])


def pack_weight(w, fmt):
    k, n = w.shape
    w = f64(bf(w)).reshape(k // 32, 32, n)
    amax = np.abs(w).max(1)
    if fmt == "e4m3":
        byte = np.frexp(amax)[1] - 1 + 127 - 7
    else:
        mant, ex = np.frexp(amax / 6.0)
        byte = np.where(mant > 0.5, ex, ex - 1) + 127
    byte = np.clip(np.where(amax > 0, byte, 1), 1, 254)
    scaled = (w * np.exp2(127.0 - byte)[:, None, :]).reshape(k, n).astype(np.float32)
    by_word = np.ascontiguousarray(scaled.reshape(k // 512, 128, 4, n).transpose(0, 1, 3, 2))
    if fmt == "e4m3":
        words = by_word.astype(ml_dtypes.float8_e4m3fn).view(np.uint8)
    else:
        c = by_word.astype(ml_dtypes.float4_e2m1fn).view(np.uint8) & 0xF
        words = c[..., 0::2] | (c[..., 1::2] << 4)
    return np.ascontiguousarray(words), np.ascontiguousarray(byte.astype(np.uint8).reshape(k // 512, 16, n))


def unpack_weight(words, scales, fmt):
    g, p, n, _ = words.shape
    if fmt == "e4m3":
        vals = np.ascontiguousarray(words).view(ml_dtypes.float8_e4m3fn).astype(np.float64)
    else:
        nib = np.empty((g, p, n, 4), np.uint8)
        nib[..., 0::2] = words & 0xF
        nib[..., 1::2] = words >> 4
        vals = E2M1[nib]
    vals = vals * np.repeat(np.exp2(scales.astype(np.float64) - 127.0), 8, axis=1)[..., None]
    return vals.transpose(0, 1, 3, 2).reshape(g * 512, n)


B, T, L, D, K = 2, 8192, 256, 1024, 128
HS = 0.25
FMT = "e4m3"


def sigmoid(v):
    return 1.0 / (1.0 + np.exp(-v))


def setup_inputs():
    s = mx_kscale(D)
    H = bf(np.random.standard_normal((B, T, D)) * HS * s)
    Wr = np.random.standard_normal((K, D)) / (HS * np.sqrt(D)) / s
    words, scales = pack_weight(np.ascontiguousarray(Wr.T), FMT)
    br = bf(np.random.standard_normal(K) * 0.3)
    return {"H": H, "Wr_words": words, "Wr_scales": scales, "br": br}


def reference(H, Wr_words, Wr_scales, br):
    h = f64(H)
    route = sigmoid((mxq(h, 2, "e4m3") @ unpack_weight(Wr_words, Wr_scales, FMT)) + f64(br))
    return mxq(route, 1, "e4m3").transpose(0, 2, 1) @ mxq(h, 1, "e4m3")

@@ -1,0 +1,231 @@
+from contextlib import ExitStack
+
+import concourse.mybir as mybir
+from concourse.masks import make_identity
+
+BF16 = mybir.dt.bfloat16
+F32 = mybir.dt.float32
+I32 = mybir.dt.int32
+U32 = mybir.dt.uint32
+U8 = mybir.dt.uint8
+FP8X4 = mybir.dt.float8_e4m3fn_x4
+SIGMOID = mybir.ActivationFunctionType.Sigmoid
+
+SEQS, FRAMES, FEATURES, SLOTS = 2, 8192, 1024, 128
+P = 128
+PACK = 4
+K_PASS = P * PACK
+BANK = 512
+
+N_GROUPS = SEQS * FRAMES // K_PASS
+GROUPS_PER_SEQ = FRAMES // K_PASS
+FEATURE_PASSES = FEATURES // K_PASS
+FEATURE_BANKS = FEATURES // BANK
+
+PREFETCH = 3
+LAG_QUANTISE = 1
+LAG_LOGITS = 2
+LAG_ROUTE_T = 3
+LAG_ROUTE_Q = 4
+LAG_POOL = 5
+
+VECTOR_COLS = 832
+
+FLOPS = 2 * 2 * SEQS * FRAMES * FEATURES * SLOTS
+
+
+def tile_instrumentspecificslotmemory_pa_k_kernel(tc, H, Wr_words, Wr_scales, br, out):
+    nc = tc.nc
+    with ExitStack() as ctx:
+        consts = ctx.enter_context(tc.tile_pool(name="consts", bufs=1))
+        h_pool = ctx.enter_context(tc.tile_pool(name="h_pool", bufs=PREFETCH + 1))
+        near = ctx.enter_context(tc.tile_pool(name="near", bufs=3))
+        far = ctx.enter_context(tc.tile_pool(name="far", bufs=LAG_POOL - LAG_QUANTISE + 2))
+        xt_pool = ctx.enter_context(tc.psum_pool(name="xt_pool", bufs=4))
+        ps_one = ctx.enter_context(tc.psum_pool(name="ps_one", bufs=1))
+
+        h_groups = H.rearrange("b (c p j) d -> (b c) p j d", p=P, j=PACK)
+
+        h = {}
+        by_feature = {}
+        feat_codes, feat_scales = {}, {}
+        logits = {}
+        route_t = {}
+        route_w = {}
+        route_codes, route_scales = {}, {}
+        by_frame = {}
+        frame_codes, frame_scales = {}, {}
+        agg = {}
+
+        def live(i):
+            return 0 <= i < N_GROUPS
+
+        def load_frames(i):
+            h[i] = h_pool.tile([P, PACK, FEATURES], BF16, name="h")
+            nc.sync.dma_start(out=h[i][:], in_=h_groups[i])
+
+        for i in range(PREFETCH):
+            load_frames(i)
+
+        warm = consts.tile([P, 2], F32, name="warm")
+        nc.vector.memset(warm[:], 0.0)
+        nc.scalar.activation(out=warm[:, 1:2], in_=warm[:, 0:1], func=SIGMOID)
+
+        ident_f32 = consts.tile([P, P], F32, name="ident_f32")
+        make_identity(nc, ident_f32[:])
+        ident_bf16 = consts.tile([P, P], BF16, name="ident_bf16")
+        make_identity(nc, ident_bf16[:])
+
+        w_words = consts.tile([P, FEATURE_PASSES, SLOTS], U32, name="w_words", align_bytes=64)
+        nc.sync.dma_start(
+            out=w_words[:].bitcast(I32),
+            in_=Wr_words.rearrange("g p n t -> p g (n t)").bitcast(I32),
+        )
+        w_scales = consts.tile([P, FEATURE_PASSES, SLOTS], U8, name="w_scales", align_bytes=64)
+        nc.vector.memset(w_scales[:].bitcast(I32), 0)
+        for quad in range(4):
+            nc.sync.dma_start(
+                out=w_scales[32 * quad : 32 * quad + 4, :, :].bitcast(I32),
+                in_=Wr_scales[:, 4 * quad : 4 * quad + 4, :].rearrange("g r n -> r g n").bitcast(I32),
+            )
+
+        bias_rows = consts.tile([P, P], BF16, name="bias_rows")
+        nc.vector.memset(bias_rows[:], 0.0)
+        nc.sync.dma_start(out=bias_rows[0:1, :], in_=br.unsqueeze(0))
+        bias_ps = ps_one.tile([P, PACK, P], BF16, name="route_ps")
+        nc.tensor.transpose(bias_ps[:, 0, :], bias_rows[:], ident_bf16[:])
+        bias = consts.tile([P, 1], F32, name="bias")
+        nc.vector.tensor_copy(out=bias[:], in_=bias_ps[:, 0, 0:1])
+
+        def regroup_frames_scalar(i):
+            by_frame[i] = near.tile([P, FEATURES, PACK], BF16, name="by_frame", align_bytes=64)
+            nc.scalar.copy(
+                out=by_frame[i][:, VECTOR_COLS:FEATURES, :].rearrange("p (c r) j -> p c j r", r=4),
+                in_=h[i][:, :, VECTOR_COLS:FEATURES].rearrange("p j (c r) -> p c j r", r=4),
+            )
+
+        def regroup_frames_vector(i):
+            nc.vector.tensor_copy(
+                out=by_frame[i][:, 0:VECTOR_COLS, :].rearrange("p (c r) j -> p c j r", r=4),
+                in_=h[i][:, :, 0:VECTOR_COLS].rearrange("p j (c r) -> p c j r", r=4),
+            )
+
+        def transpose_features(i, g):
+            if g == 0:
+                by_feature[i] = near.tile([P, FEATURE_PASSES, K_PASS, PACK], BF16, name="by_feature", align_bytes=64)
+            for half in range(2):
+                xt = xt_pool.tile([P, 2, 2, P], F32, name="xt")
+                for jj in range(2):
+                    words = h[i][:, 2 * half + jj, :].bitcast(F32)
+                    for u in range(2):
+                        nc.tensor.transpose(
+                            xt[:, jj, u, :],
+                            words[:, 256 * g + u : 256 * (g + 1) : 2],
+                            ident_f32[:],
+                        )
+                dst = by_feature[i][:, g, 256 * half : 256 * (half + 1), :]
+                nc.scalar.copy(
+                    out=dst.rearrange("p n t -> p (n t)").bitcast(F32).rearrange("p (jj n u) -> p jj n u", jj=2, u=2),
+                    in_=xt[:].rearrange("p jj u n -> p jj n u"),
+                )
+
+        def quantise_features(i):
+            feat_codes[i] = near.tile([P, FEATURE_PASSES, K_PASS], U32, name="feat_codes", align_bytes=64)
+            feat_scales[i] = near.tile([P, FEATURE_PASSES, K_PASS], U8, name="feat_scales", align_bytes=64)
+            for g in range(FEATURE_PASSES):
+                nc.vector.quantize_mx(
+                    out=feat_codes[i][:, g, :].bitcast(FP8X4),
+                    scales=feat_scales[i][:, g, :],
+                    in_=by_feature[i][:, g, :, :].rearrange("p n t -> p (n t)"),
+                )
+
+        def route_logits(i):
+            logits[i] = ps_one.tile([P, K_PASS], F32, name="logits")
+            for g in range(FEATURE_PASSES):
+                nc.tensor.matmul_mx(
+                    out=logits[i][:],
+                    lhsT=w_words[:, g, :].bitcast(FP8X4),
+                    lhsT_scale=w_scales[:, g, :],
+                    rhs=feat_codes[i][:, g, :].bitcast(FP8X4),
+                    rhs_scale=feat_scales[i][:, g, :],
+                    start=(g == 0),
+                    stop=(g == FEATURE_PASSES - 1),
+                )
+
+        def route_sigmoid(i):
+            route_t[i] = near.tile([P, K_PASS], BF16, name="route_t")
+            nc.scalar.activation(out=route_t[i][:], in_=logits[i][:], func=SIGMOID, bias=bias[:], scale=1.0)
+
+        def transpose_route(i):
+            route_ps = ps_one.tile([P, PACK, P], BF16, name="route_ps")
+            for j in range(PACK):
+                nc.tensor.transpose(route_ps[:, j, :], route_t[i][:, P * j : P * (j + 1)], ident_bf16[:])
+            route_w[i] = near.tile([P, SLOTS, PACK], BF16, name="route_w", align_bytes=64)
+            nc.scalar.copy(out=route_w[i][:], in_=route_ps[:].rearrange("p j k -> p k j"))
+
+        def quantise_route(i):
+            route_codes[i] = near.tile([P, SLOTS], U32, name="route_codes", align_bytes=64)
+            route_scales[i] = near.tile([P, SLOTS], U8, name="route_scales", align_bytes=64)
+            nc.vector.quantize_mx(
+                out=route_codes[i][:].bitcast(FP8X4),
+                scales=route_scales[i][:],
+                in_=route_w[i][:].rearrange("p k j -> p (k j)"),
+            )
+
+        def quantise_frames(i):
+            frame_codes[i] = far.tile([P, FEATURES], U32, name="frame_codes", align_bytes=64)
+            frame_scales[i] = far.tile([P, FEATURES], U8, name="frame_scales", align_bytes=64)
+            nc.vector.quantize_mx(
+                out=frame_codes[i][:].bitcast(FP8X4),
+                scales=frame_scales[i][:],
+                in_=by_frame[i][:].rearrange("p d j -> p (d j)"),
+            )
+
+        def pool_frames(i):
+            seq, c = divmod(i, GROUPS_PER_SEQ)
+            for b in range(FEATURE_BANKS):
+                if c == 0:
+                    agg[b] = ps_one.tile([P, BANK], F32, name="agg%d" % b)
+                nc.tensor.matmul_mx(
+                    out=agg[b][:],
+                    lhsT=route_codes[i][:].bitcast(FP8X4),
+                    lhsT_scale=route_scales[i][:],
+                    rhs=frame_codes[i][:, BANK * b : BANK * (b + 1)].bitcast(FP8X4),
+                    rhs_scale=frame_scales[i][:, BANK * b : BANK * (b + 1)],
+                    start=(c == 0),
+                    stop=(c == GROUPS_PER_SEQ - 1),
+                )
+            if c == GROUPS_PER_SEQ - 1:
+                result = near.tile([P, FEATURES], F32, name="result")
+                nc.scalar.copy(out=result[:, 0:BANK], in_=agg[0][:])
+                nc.vector.tensor_copy(out=result[:, BANK : 2 * BANK], in_=agg[1][:])
+                for b in range(FEATURE_BANKS):
+                    nc.sync.dma_start(
+                        out=out[seq, :, BANK * b : BANK * (b + 1)], in_=result[:, BANK * b : BANK * (b + 1)]
+                    )
+
+        with tc.manual_schedule():
+            for n in range(N_GROUPS + LAG_POOL):
+                if live(n + PREFETCH):
+                    load_frames(n + PREFETCH)
+                if live(n):
+                    regroup_frames_scalar(n)
+                    transpose_features(n, 0)
+                if live(n - LAG_LOGITS):
+                    route_logits(n - LAG_LOGITS)
+                if live(n):
+                    transpose_features(n, 1)
+                if live(n - LAG_LOGITS):
+                    route_sigmoid(n - LAG_LOGITS)
+                if live(n - LAG_ROUTE_T):
+                    transpose_route(n - LAG_ROUTE_T)
+                if live(n - LAG_QUANTISE):
+                    quantise_features(n - LAG_QUANTISE)
+                if live(n - LAG_ROUTE_Q):
+                    quantise_route(n - LAG_ROUTE_Q)
+                if live(n - LAG_QUANTISE):
+                    quantise_frames(n - LAG_QUANTISE)
+                if live(n):
+                    regroup_frames_vector(n)
+                if live(n - LAG_POOL):
+                    pool_frames(n - LAG_POOL)

@@ -29,7 +29,7 @@ LAG_ROUTE_T = 3
 LAG_ROUTE_Q = 4
 LAG_POOL = 5
 
-VECTOR_COLS = 832
+VECTOR_COLS = 768
 
 FLOPS = 2 * 2 * SEQS * FRAMES * FEATURES * SLOTS
 

@@ -15,7 +15,11 @@ SEQS, FRAMES, FEATURES, SLOTS = 2, 8192, 1024, 128
 P = 128
 PACK = 4
 K_PASS = P * PACK
+PAIR = 2
+PASS_WORDS = K_PASS // PAIR
 BANK = 512
+ROWS_PER_BANK = BANK // (PAIR * P)
+QUADRANT = 32
 
 N_GROUPS = SEQS * FRAMES // K_PASS
 GROUPS_PER_SEQ = FRAMES // K_PASS
@@ -29,7 +33,8 @@ LAG_ROUTE_T = 3
 LAG_ROUTE_Q = 4
 LAG_POOL = 5
 
-VECTOR_COLS = 768
+VECTOR_COLS = 792
+RUN = 4
 
 FLOPS = 2 * 2 * SEQS * FRAMES * FEATURES * SLOTS
 
@@ -47,14 +52,9 @@ def tile_instrumentspecificslotmemory_pa_k_kernel(tc, H, Wr_words, Wr_scales, br
         h_groups = H.rearrange("b (c p j) d -> (b c) p j d", p=P, j=PACK)
 
         h = {}
-        by_feature = {}
-        feat_codes, feat_scales = {}, {}
-        logits = {}
-        route_t = {}
-        route_w = {}
-        route_codes, route_scales = {}, {}
-        by_frame = {}
-        frame_codes, frame_scales = {}, {}
+        by_feature, feature_codes, feature_scales = {}, {}, {}
+        logits, route_t, route_w, route_codes, route_scales = {}, {}, {}, {}, {}
+        by_frame, frame_codes, frame_scales = {}, {}, {}
         agg = {}
 
         def live(i):
@@ -83,9 +83,9 @@ def tile_instrumentspecificslotmemory_pa_k_kernel(tc, H, Wr_words, Wr_scales, br
         )
         w_scales = consts.tile([P, FEATURE_PASSES, SLOTS], U8, name="w_scales", align_bytes=64)
         nc.vector.memset(w_scales[:].bitcast(I32), 0)
-        for quad in range(4):
+        for quad in range(P // QUADRANT):
             nc.sync.dma_start(
-                out=w_scales[32 * quad : 32 * quad + 4, :, :].bitcast(I32),
+                out=w_scales[QUADRANT * quad : QUADRANT * quad + 4, :, :].bitcast(I32),
                 in_=Wr_scales[:, 4 * quad : 4 * quad + 4, :].rearrange("g r n -> r g n").bitcast(I32),
             )
 
@@ -100,42 +100,44 @@ def tile_instrumentspecificslotmemory_pa_k_kernel(tc, H, Wr_words, Wr_scales, br
         def regroup_frames_scalar(i):
             by_frame[i] = near.tile([P, FEATURES, PACK], BF16, name="by_frame", align_bytes=64)
             nc.scalar.copy(
-                out=by_frame[i][:, VECTOR_COLS:FEATURES, :].rearrange("p (c r) j -> p c j r", r=4),
-                in_=h[i][:, :, VECTOR_COLS:FEATURES].rearrange("p j (c r) -> p c j r", r=4),
+                out=by_frame[i][:, VECTOR_COLS:FEATURES, :].rearrange("p (c r) j -> p c j r", r=RUN),
+                in_=h[i][:, :, VECTOR_COLS:FEATURES].rearrange("p j (c r) -> p c j r", r=RUN),
             )
 
         def regroup_frames_vector(i):
             nc.vector.tensor_copy(
-                out=by_frame[i][:, 0:VECTOR_COLS, :].rearrange("p (c r) j -> p c j r", r=4),
-                in_=h[i][:, :, 0:VECTOR_COLS].rearrange("p j (c r) -> p c j r", r=4),
+                out=by_frame[i][:, 0:VECTOR_COLS, :].rearrange("p (c r) j -> p c j r", r=RUN),
+                in_=h[i][:, :, 0:VECTOR_COLS].rearrange("p j (c r) -> p c j r", r=RUN),
             )
 
         def transpose_features(i, g):
             if g == 0:
                 by_feature[i] = near.tile([P, FEATURE_PASSES, K_PASS, PACK], BF16, name="by_feature", align_bytes=64)
-            for half in range(2):
-                xt = xt_pool.tile([P, 2, 2, P], F32, name="xt")
-                for jj in range(2):
-                    words = h[i][:, 2 * half + jj, :].bitcast(F32)
-                    for u in range(2):
+            for j0 in range(0, PACK, ROWS_PER_BANK):
+                xt = xt_pool.tile([P, ROWS_PER_BANK, PAIR, P], F32, name="xt")
+                for r in range(ROWS_PER_BANK):
+                    words = h[i][:, j0 + r, :].bitcast(F32)
+                    for u in range(PAIR):
                         nc.tensor.transpose(
-                            xt[:, jj, u, :],
-                            words[:, 256 * g + u : 256 * (g + 1) : 2],
+                            xt[:, r, u, :],
+                            words[:, PASS_WORDS * g + u : PASS_WORDS * (g + 1) : PAIR],
                             ident_f32[:],
                         )
-                dst = by_feature[i][:, g, 256 * half : 256 * (half + 1), :]
+                columns = by_feature[i][:, g, P * j0 : P * (j0 + ROWS_PER_BANK), :]
                 nc.scalar.copy(
-                    out=dst.rearrange("p n t -> p (n t)").bitcast(F32).rearrange("p (jj n u) -> p jj n u", jj=2, u=2),
-                    in_=xt[:].rearrange("p jj u n -> p jj n u"),
+                    out=columns.rearrange("p n t -> p (n t)")
+                    .bitcast(F32)
+                    .rearrange("p (r n u) -> p r n u", r=ROWS_PER_BANK, u=PAIR),
+                    in_=xt[:].rearrange("p r u n -> p r n u"),
                 )
 
         def quantise_features(i):
-            feat_codes[i] = near.tile([P, FEATURE_PASSES, K_PASS], U32, name="feat_codes", align_bytes=64)
-            feat_scales[i] = near.tile([P, FEATURE_PASSES, K_PASS], U8, name="feat_scales", align_bytes=64)
+            feature_codes[i] = near.tile([P, FEATURE_PASSES, K_PASS], U32, name="feature_codes", align_bytes=64)
+            feature_scales[i] = near.tile([P, FEATURE_PASSES, K_PASS], U8, name="feature_scales", align_bytes=64)
             for g in range(FEATURE_PASSES):
                 nc.vector.quantize_mx(
-                    out=feat_codes[i][:, g, :].bitcast(FP8X4),
-                    scales=feat_scales[i][:, g, :],
+                    out=feature_codes[i][:, g, :].bitcast(FP8X4),
+                    scales=feature_scales[i][:, g, :],
                     in_=by_feature[i][:, g, :, :].rearrange("p n t -> p (n t)"),
                 )
 
@@ -146,8 +148,8 @@ def tile_instrumentspecificslotmemory_pa_k_kernel(tc, H, Wr_words, Wr_scales, br
                     out=logits[i][:],
                     lhsT=w_words[:, g, :].bitcast(FP8X4),
                     lhsT_scale=w_scales[:, g, :],
-                    rhs=feat_codes[i][:, g, :].bitcast(FP8X4),
-                    rhs_scale=feat_scales[i][:, g, :],
+                    rhs=feature_codes[i][:, g, :].bitcast(FP8X4),
+                    rhs_scale=feature_scales[i][:, g, :],
                     start=(g == 0),
                     stop=(g == FEATURE_PASSES - 1),
                 )

@@ -33,7 +33,7 @@ LAG_ROUTE_T = 3
 LAG_ROUTE_Q = 4
 LAG_POOL = 5
 
-VECTOR_COLS = 792
+VECTOR_COLS = 752
 RUN = 4
 
 FLOPS = 2 * 2 * SEQS * FRAMES * FEATURES * SLOTS
@@ -156,14 +156,24 @@ def tile_instrumentspecificslotmemory_pa_k_kernel(tc, H, Wr_words, Wr_scales, br
 
         def route_sigmoid(i):
             route_t[i] = near.tile([P, K_PASS], BF16, name="route_t")
-            nc.scalar.activation(out=route_t[i][:], in_=logits[i][:], func=SIGMOID, bias=bias[:], scale=1.0)
+            nc.scalar.activation(
+                out=route_t[i][:].rearrange("s (u p e) -> s u p e", u=PAIR, e=PAIR),
+                in_=logits[i][:].rearrange("s (u e p) -> s u p e", u=PAIR, e=PAIR),
+                func=SIGMOID,
+                bias=bias[:],
+                scale=1.0,
+            )
 
         def transpose_route(i):
-            route_ps = ps_one.tile([P, PACK, P], BF16, name="route_ps")
-            for j in range(PACK):
-                nc.tensor.transpose(route_ps[:, j, :], route_t[i][:, P * j : P * (j + 1)], ident_bf16[:])
+            route_ps = ps_one.tile([P, PAIR, P], F32, name="route_ps")
+            words = route_t[i][:].bitcast(F32)
+            for u in range(PAIR):
+                nc.tensor.transpose(route_ps[:, u, :], words[:, P * u : P * (u + 1)], ident_f32[:])
             route_w[i] = near.tile([P, SLOTS, PACK], BF16, name="route_w", align_bytes=64)
-            nc.scalar.copy(out=route_w[i][:], in_=route_ps[:].rearrange("p j k -> p k j"))
+            nc.scalar.copy(
+                out=route_w[i][:].rearrange("p k j -> p (k j)").bitcast(F32).rearrange("p (k u) -> p k u", u=PAIR),
+                in_=route_ps[:].rearrange("p u k -> p k u"),
+            )
 
         def quantise_route(i):
             route_codes[i] = near.tile([P, SLOTS], U32, name="route_codes", align_bytes=64)

@@ -28,12 +28,16 @@ FEATURE_BANKS = FEATURES // BANK
 
 PREFETCH = 3
 LAG_QUANTISE = 1
+LAG_FRAMES_Q = 2
 LAG_LOGITS = 2
 LAG_ROUTE_T = 3
 LAG_ROUTE_Q = 4
 LAG_POOL = 5
+LAG_STORE = 6
 
-VECTOR_COLS = 752
+VECTOR_COLS = 784
+FIRST_VECTOR_COLS = FEATURES
+LAST_VECTOR_COLS = FEATURES // 2
 RUN = 4
 
 FLOPS = 2 * 2 * SEQS * FRAMES * FEATURES * SLOTS
@@ -43,9 +47,11 @@ def tile_instrumentspecificslotmemory_pa_k_kernel(tc, H, Wr_words, Wr_scales, br
     nc = tc.nc
     with ExitStack() as ctx:
         consts = ctx.enter_context(tc.tile_pool(name="consts", bufs=1))
+        h_first = ctx.enter_context(tc.tile_pool(name="h_first", bufs=FEATURES // K_PASS))
         h_pool = ctx.enter_context(tc.tile_pool(name="h_pool", bufs=PREFETCH + 1))
         near = ctx.enter_context(tc.tile_pool(name="near", bufs=3))
-        far = ctx.enter_context(tc.tile_pool(name="far", bufs=LAG_POOL - LAG_QUANTISE + 2))
+        frames = ctx.enter_context(tc.tile_pool(name="frames", bufs=LAG_FRAMES_Q + 2))
+        far = ctx.enter_context(tc.tile_pool(name="far", bufs=LAG_POOL - LAG_FRAMES_Q + 2))
         xt_pool = ctx.enter_context(tc.psum_pool(name="xt_pool", bufs=4))
         ps_one = ctx.enter_context(tc.psum_pool(name="ps_one", bufs=1))
 
@@ -60,9 +66,24 @@ def tile_instrumentspecificslotmemory_pa_k_kernel(tc, H, Wr_words, Wr_scales, br
         def live(i):
             return 0 <= i < N_GROUPS
 
+        def piece_width(i):
+            return K_PASS if i == 0 else FEATURES
+
+        def frames_of(i, start, stop):
+            width = piece_width(i)
+            k = start // width
+            return h[i][k][:, :, start - k * width : stop - k * width]
+
         def load_frames(i):
-            h[i] = h_pool.tile([P, PACK, FEATURES], BF16, name="h")
-            nc.sync.dma_start(out=h[i][:], in_=h_groups[i])
+            width = piece_width(i)
+            h[i] = []
+            for start in range(0, FEATURES, width):
+                if width == FEATURES:
+                    piece = h_pool.tile([P, PACK, FEATURES], BF16, name="h")
+                else:
+                    piece = h_first.tile([P, PACK, K_PASS], BF16, name="h_half")
+                nc.sync.dma_start(out=piece[:], in_=h_groups[i][:, :, start : start + width])
+                h[i].append(piece)
 
         for i in range(PREFETCH):
             load_frames(i)
@@ -97,18 +118,28 @@ def tile_instrumentspecificslotmemory_pa_k_kernel(tc, H, Wr_words, Wr_scales, br
         bias = consts.tile([P, 1], F32, name="bias")
         nc.vector.tensor_copy(out=bias[:], in_=bias_ps[:, 0, 0:1])
 
+        def vector_cols(i):
+            if i == 0:
+                return FIRST_VECTOR_COLS
+            return LAST_VECTOR_COLS if i == N_GROUPS - 1 else VECTOR_COLS
+
         def regroup_frames_scalar(i):
-            by_frame[i] = near.tile([P, FEATURES, PACK], BF16, name="by_frame", align_bytes=64)
-            nc.scalar.copy(
-                out=by_frame[i][:, VECTOR_COLS:FEATURES, :].rearrange("p (c r) j -> p c j r", r=RUN),
-                in_=h[i][:, :, VECTOR_COLS:FEATURES].rearrange("p j (c r) -> p c j r", r=RUN),
-            )
+            by_frame[i] = frames.tile([P, FEATURES, PACK], BF16, name="by_frame", align_bytes=64)
+            cols = vector_cols(i)
+            if cols < FEATURES:
+                nc.scalar.copy(
+                    out=by_frame[i][:, cols:FEATURES, :].rearrange("p (c r) j -> p c j r", r=RUN),
+                    in_=frames_of(i, cols, FEATURES).rearrange("p j (c r) -> p c j r", r=RUN),
+                )
 
         def regroup_frames_vector(i):
-            nc.vector.tensor_copy(
-                out=by_frame[i][:, 0:VECTOR_COLS, :].rearrange("p (c r) j -> p c j r", r=RUN),
-                in_=h[i][:, :, 0:VECTOR_COLS].rearrange("p j (c r) -> p c j r", r=RUN),
-            )
+            cols = vector_cols(i)
+            step = min(cols, piece_width(i))
+            for start in range(0, cols, step):
+                nc.vector.tensor_copy(
+                    out=by_frame[i][:, start : start + step, :].rearrange("p (c r) j -> p c j r", r=RUN),
+                    in_=frames_of(i, start, start + step).rearrange("p j (c r) -> p c j r", r=RUN),
+                )
 
         def transpose_features(i, g):
             if g == 0:
@@ -116,11 +147,11 @@ def tile_instrumentspecificslotmemory_pa_k_kernel(tc, H, Wr_words, Wr_scales, br
             for j0 in range(0, PACK, ROWS_PER_BANK):
                 xt = xt_pool.tile([P, ROWS_PER_BANK, PAIR, P], F32, name="xt")
                 for r in range(ROWS_PER_BANK):
-                    words = h[i][:, j0 + r, :].bitcast(F32)
+                    words = frames_of(i, K_PASS * g, K_PASS * (g + 1))[:, j0 + r, :].bitcast(F32)
                     for u in range(PAIR):
                         nc.tensor.transpose(
                             xt[:, r, u, :],
-                            words[:, PASS_WORDS * g + u : PASS_WORDS * (g + 1) : PAIR],
+                            words[:, u:PASS_WORDS:PAIR],
                             ident_f32[:],
                         )
                 columns = by_feature[i][:, g, P * j0 : P * (j0 + ROWS_PER_BANK), :]
@@ -207,6 +238,9 @@ def tile_instrumentspecificslotmemory_pa_k_kernel(tc, H, Wr_words, Wr_scales, br
                     start=(c == 0),
                     stop=(c == GROUPS_PER_SEQ - 1),
                 )
+
+        def store_sums(i):
+            seq, c = divmod(i, GROUPS_PER_SEQ)
             if c == GROUPS_PER_SEQ - 1:
                 result = near.tile([P, FEATURES], F32, name="result")
                 nc.scalar.copy(out=result[:, 0:BANK], in_=agg[0][:])
@@ -216,12 +250,16 @@ def tile_instrumentspecificslotmemory_pa_k_kernel(tc, H, Wr_words, Wr_scales, br
                         out=out[seq, :, BANK * b : BANK * (b + 1)], in_=result[:, BANK * b : BANK * (b + 1)]
                     )
 
+        last = N_GROUPS - 1
         with tc.manual_schedule():
-            for n in range(N_GROUPS + LAG_POOL):
+            for n in range(N_GROUPS + LAG_STORE):
                 if live(n + PREFETCH):
                     load_frames(n + PREFETCH)
-                if live(n):
+                if live(n) and n < last:
                     regroup_frames_scalar(n)
+                if live(n - LAG_STORE):
+                    store_sums(n - LAG_STORE)
+                if live(n):
                     transpose_features(n, 0)
                 if live(n - LAG_LOGITS):
                     route_logits(n - LAG_LOGITS)
@@ -231,13 +269,17 @@ def tile_instrumentspecificslotmemory_pa_k_kernel(tc, H, Wr_words, Wr_scales, br
                     route_sigmoid(n - LAG_LOGITS)
                 if live(n - LAG_ROUTE_T):
                     transpose_route(n - LAG_ROUTE_T)
+                if n == last:
+                    regroup_frames_scalar(n)
                 if live(n - LAG_QUANTISE):
                     quantise_features(n - LAG_QUANTISE)
                 if live(n - LAG_ROUTE_Q):
                     quantise_route(n - LAG_ROUTE_Q)
-                if live(n - LAG_QUANTISE):
-                    quantise_frames(n - LAG_QUANTISE)
-                if live(n):
+                if live(n - LAG_FRAMES_Q):
+                    quantise_frames(n - LAG_FRAMES_Q)
+                if live(n) and n < last:
                     regroup_frames_vector(n)
+                if n == last + 1:
+                    regroup_frames_vector(last)
                 if live(n - LAG_POOL):
                     pool_frames(n - LAG_POOL)

@@ -35,7 +35,7 @@ LAG_ROUTE_Q = 4
 LAG_POOL = 5
 LAG_STORE = 6
 
-VECTOR_COLS = 784
+VECTOR_COLS = 760
 FIRST_VECTOR_COLS = FEATURES
 LAST_VECTOR_COLS = FEATURES // 2
 RUN = 4

@@ -33,11 +33,10 @@ LAG_LOGITS = 2
 LAG_ROUTE_T = 3
 LAG_ROUTE_Q = 4
 LAG_POOL = 5
-LAG_STORE = 6
+NEW_SEQ_LAG = 1
 
-VECTOR_COLS = 760
-FIRST_VECTOR_COLS = FEATURES
-LAST_VECTOR_COLS = FEATURES // 2
+VECTOR_COLS = 752
+LAST_PIECE = FEATURES // 4
 RUN = 4
 
 FLOPS = 2 * 2 * SEQS * FRAMES * FEATURES * SLOTS
@@ -51,7 +50,7 @@ def tile_instrumentspecificslotmemory_pa_k_kernel(tc, H, Wr_words, Wr_scales, br
         h_pool = ctx.enter_context(tc.tile_pool(name="h_pool", bufs=PREFETCH + 1))
         near = ctx.enter_context(tc.tile_pool(name="near", bufs=3))
         frames = ctx.enter_context(tc.tile_pool(name="frames", bufs=LAG_FRAMES_Q + 2))
-        far = ctx.enter_context(tc.tile_pool(name="far", bufs=LAG_POOL - LAG_FRAMES_Q + 2))
+        far = ctx.enter_context(tc.tile_pool(name="far", bufs=LAG_POOL + NEW_SEQ_LAG - LAG_FRAMES_Q + 2))
         xt_pool = ctx.enter_context(tc.psum_pool(name="xt_pool", bufs=4))
         ps_one = ctx.enter_context(tc.psum_pool(name="ps_one", bufs=1))
 
@@ -80,9 +79,14 @@ def tile_instrumentspecificslotmemory_pa_k_kernel(tc, H, Wr_words, Wr_scales, br
             for start in range(0, FEATURES, width):
                 if width == FEATURES:
                     piece = h_pool.tile([P, PACK, FEATURES], BF16, name="h")
+                    rows = PACK
                 else:
                     piece = h_first.tile([P, PACK, K_PASS], BF16, name="h_half")
-                nc.sync.dma_start(out=piece[:], in_=h_groups[i][:, :, start : start + width])
+                    rows = ROWS_PER_BANK
+                for j0 in range(0, PACK, rows):
+                    nc.sync.dma_start(
+                        out=piece[:, j0 : j0 + rows, :], in_=h_groups[i][:, j0 : j0 + rows, start : start + width]
+                    )
                 h[i].append(piece)
 
         for i in range(PREFETCH):
@@ -118,28 +122,17 @@ def tile_instrumentspecificslotmemory_pa_k_kernel(tc, H, Wr_words, Wr_scales, br
         bias = consts.tile([P, 1], F32, name="bias")
         nc.vector.tensor_copy(out=bias[:], in_=bias_ps[:, 0, 0:1])
 
-        def vector_cols(i):
-            if i == 0:
-                return FIRST_VECTOR_COLS
-            return LAST_VECTOR_COLS if i == N_GROUPS - 1 else VECTOR_COLS
+        def regroup(copy, i, start, stop):
+            if i not in by_frame:
+                by_frame[i] = frames.tile([P, FEATURES, PACK], BF16, name="by_frame", align_bytes=64)
+            copy(
+                out=by_frame[i][:, start:stop, :].rearrange("p (c r) j -> p c j r", r=RUN),
+                in_=frames_of(i, start, stop).rearrange("p j (c r) -> p c j r", r=RUN),
+            )
 
-        def regroup_frames_scalar(i):
-            by_frame[i] = frames.tile([P, FEATURES, PACK], BF16, name="by_frame", align_bytes=64)
-            cols = vector_cols(i)
-            if cols < FEATURES:
-                nc.scalar.copy(
-                    out=by_frame[i][:, cols:FEATURES, :].rearrange("p (c r) j -> p c j r", r=RUN),
-                    in_=frames_of(i, cols, FEATURES).rearrange("p j (c r) -> p c j r", r=RUN),
-                )
-
-        def regroup_frames_vector(i):
-            cols = vector_cols(i)
-            step = min(cols, piece_width(i))
-            for start in range(0, cols, step):
-                nc.vector.tensor_copy(
-                    out=by_frame[i][:, start : start + step, :].rearrange("p (c r) j -> p c j r", r=RUN),
-                    in_=frames_of(i, start, start + step).rearrange("p j (c r) -> p c j r", r=RUN),
-                )
+        def regroup_last(pieces):
+            for k in pieces:
+                regroup(nc.scalar.copy, N_GROUPS - 1, LAST_PIECE * k, LAST_PIECE * (k + 1))
 
         def transpose_features(i, g):
             if g == 0:
@@ -239,47 +232,51 @@ def tile_instrumentspecificslotmemory_pa_k_kernel(tc, H, Wr_words, Wr_scales, br
                     stop=(c == GROUPS_PER_SEQ - 1),
                 )
 
-        def store_sums(i):
-            seq, c = divmod(i, GROUPS_PER_SEQ)
-            if c == GROUPS_PER_SEQ - 1:
-                result = near.tile([P, FEATURES], F32, name="result")
-                nc.scalar.copy(out=result[:, 0:BANK], in_=agg[0][:])
-                nc.vector.tensor_copy(out=result[:, BANK : 2 * BANK], in_=agg[1][:])
-                for b in range(FEATURE_BANKS):
-                    nc.sync.dma_start(
-                        out=out[seq, :, BANK * b : BANK * (b + 1)], in_=result[:, BANK * b : BANK * (b + 1)]
-                    )
+        def pool_round(i):
+            return i + LAG_POOL + NEW_SEQ_LAG * (i // GROUPS_PER_SEQ)
+
+        def empty_bank(seq, b, copy):
+            result = near.tile([P, BANK], F32, name="result")
+            copy(out=result[:], in_=agg[b][:])
+            nc.sync.dma_start(out=out[seq, :, BANK * b : BANK * (b + 1)], in_=result[:])
 
         last = N_GROUPS - 1
         with tc.manual_schedule():
-            for n in range(N_GROUPS + LAG_STORE):
+            for n in range(pool_round(last) + 2):
+                finished = [k for k in range(SEQS) if pool_round(GROUPS_PER_SEQ * (k + 1) - 1) == n - 1]
                 if live(n + PREFETCH):
                     load_frames(n + PREFETCH)
-                if live(n) and n < last:
-                    regroup_frames_scalar(n)
-                if live(n - LAG_STORE):
-                    store_sums(n - LAG_STORE)
+                if 0 < n < last:
+                    regroup(nc.scalar.copy, n, VECTOR_COLS, FEATURES)
                 if live(n):
                     transpose_features(n, 0)
                 if live(n - LAG_LOGITS):
                     route_logits(n - LAG_LOGITS)
                 if live(n):
                     transpose_features(n, 1)
+                for seq in finished:
+                    empty_bank(seq, 0, nc.scalar.copy)
                 if live(n - LAG_LOGITS):
                     route_sigmoid(n - LAG_LOGITS)
                 if live(n - LAG_ROUTE_T):
                     transpose_route(n - LAG_ROUTE_T)
                 if n == last:
-                    regroup_frames_scalar(n)
+                    regroup_last((0, 1))
+                if n == last + 1:
+                    regroup_last((2, 3))
                 if live(n - LAG_QUANTISE):
                     quantise_features(n - LAG_QUANTISE)
+                for seq in finished:
+                    empty_bank(seq, 1, nc.vector.tensor_copy)
                 if live(n - LAG_ROUTE_Q):
                     quantise_route(n - LAG_ROUTE_Q)
                 if live(n - LAG_FRAMES_Q):
                     quantise_frames(n - LAG_FRAMES_Q)
-                if live(n) and n < last:
-                    regroup_frames_vector(n)
-                if n == last + 1:
-                    regroup_frames_vector(last)
-                if live(n - LAG_POOL):
-                    pool_frames(n - LAG_POOL)
+                if n == 0:
+                    for start in range(0, FEATURES, K_PASS):
+                        regroup(nc.vector.tensor_copy, n, start, start + K_PASS)
+                elif n < last:
+                    regroup(nc.vector.tensor_copy, n, 0, VECTOR_COLS)
+                for i in range(N_GROUPS):
+                    if pool_round(i) == n:
+                        pool_frames(i)

@@ -35,9 +35,9 @@ LAG_ROUTE_Q = 4
 LAG_POOL = 5
 NEW_SEQ_LAG = 1
 
-VECTOR_COLS = 752
-LAST_PIECE = FEATURES // 4
-RUN = 4
+VECTOR_COLS = 760
+LAST_VECTOR_COLS = FEATURES // 2
+RUN = 8
 
 FLOPS = 2 * 2 * SEQS * FRAMES * FEATURES * SLOTS
 
@@ -129,10 +129,6 @@ def tile_instrumentspecificslotmemory_pa_k_kernel(tc, H, Wr_words, Wr_scales, br
                 out=by_frame[i][:, start:stop, :].rearrange("p (c r) j -> p c j r", r=RUN),
                 in_=frames_of(i, start, stop).rearrange("p j (c r) -> p c j r", r=RUN),
             )
-
-        def regroup_last(pieces):
-            for k in pieces:
-                regroup(nc.scalar.copy, N_GROUPS - 1, LAST_PIECE * k, LAST_PIECE * (k + 1))
 
         def transpose_features(i, g):
             if g == 0:
@@ -261,9 +257,7 @@ def tile_instrumentspecificslotmemory_pa_k_kernel(tc, H, Wr_words, Wr_scales, br
                 if live(n - LAG_ROUTE_T):
                     transpose_route(n - LAG_ROUTE_T)
                 if n == last:
-                    regroup_last((0, 1))
-                if n == last + 1:
-                    regroup_last((2, 3))
+                    regroup(nc.scalar.copy, n, LAST_VECTOR_COLS, FEATURES)
                 if live(n - LAG_QUANTISE):
                     quantise_features(n - LAG_QUANTISE)
                 for seq in finished:
@@ -277,6 +271,8 @@ def tile_instrumentspecificslotmemory_pa_k_kernel(tc, H, Wr_words, Wr_scales, br
                         regroup(nc.vector.tensor_copy, n, start, start + K_PASS)
                 elif n < last:
                     regroup(nc.vector.tensor_copy, n, 0, VECTOR_COLS)
+                elif n == last + 1:
+                    regroup(nc.vector.tensor_copy, last, 0, LAST_VECTOR_COLS)
                 for i in range(N_GROUPS):
                     if pool_round(i) == n:
                         pool_frames(i)

from contextlib import ExitStack

import concourse.mybir as mybir
from concourse.masks import make_identity

BF16 = mybir.dt.bfloat16
F32 = mybir.dt.float32
I32 = mybir.dt.int32
U32 = mybir.dt.uint32
U8 = mybir.dt.uint8
FP8X4 = mybir.dt.float8_e4m3fn_x4
SIGMOID = mybir.ActivationFunctionType.Sigmoid

SEQS, FRAMES, FEATURES, SLOTS = 2, 8192, 1024, 128
P = 128
PACK = 4
K_PASS = P * PACK
PAIR = 2
PASS_WORDS = K_PASS // PAIR
BANK = 512
ROWS_PER_BANK = BANK // (PAIR * P)
QUADRANT = 32

N_GROUPS = SEQS * FRAMES // K_PASS
GROUPS_PER_SEQ = FRAMES // K_PASS
FEATURE_PASSES = FEATURES // K_PASS
FEATURE_BANKS = FEATURES // BANK

PREFETCH = 3
LAG_QUANTISE = 1
LAG_FRAMES_Q = 2
LAG_LOGITS = 2
LAG_ROUTE_T = 3
LAG_ROUTE_Q = 4
LAG_POOL = 5
NEW_SEQ_LAG = 1

VECTOR_COLS = 760
LAST_VECTOR_COLS = FEATURES // 2
RUN = 8

FLOPS = 2 * 2 * SEQS * FRAMES * FEATURES * SLOTS


def tile_instrumentspecificslotmemory_pa_k_kernel(tc, H, Wr_words, Wr_scales, br, out):
    nc = tc.nc
    with ExitStack() as ctx:
        consts = ctx.enter_context(tc.tile_pool(name="consts", bufs=1))
        h_first = ctx.enter_context(tc.tile_pool(name="h_first", bufs=FEATURES // K_PASS))
        h_pool = ctx.enter_context(tc.tile_pool(name="h_pool", bufs=PREFETCH + 1))
        near = ctx.enter_context(tc.tile_pool(name="near", bufs=3))
        frames = ctx.enter_context(tc.tile_pool(name="frames", bufs=LAG_FRAMES_Q + 2))
        far = ctx.enter_context(tc.tile_pool(name="far", bufs=LAG_POOL + NEW_SEQ_LAG - LAG_FRAMES_Q + 2))
        xt_pool = ctx.enter_context(tc.psum_pool(name="xt_pool", bufs=4))
        ps_one = ctx.enter_context(tc.psum_pool(name="ps_one", bufs=1))

        h_groups = H.rearrange("b (c p j) d -> (b c) p j d", p=P, j=PACK)

        h = {}
        by_feature, feature_codes, feature_scales = {}, {}, {}
        logits, route_t, route_w, route_codes, route_scales = {}, {}, {}, {}, {}
        by_frame, frame_codes, frame_scales = {}, {}, {}
        agg = {}

        def live(i):
            return 0 <= i < N_GROUPS

        def piece_width(i):
            return K_PASS if i == 0 else FEATURES

        def frames_of(i, start, stop):
            width = piece_width(i)
            k = start // width
            return h[i][k][:, :, start - k * width : stop - k * width]

        def load_frames(i):
            width = piece_width(i)
            h[i] = []
            for start in range(0, FEATURES, width):
                if width == FEATURES:
                    piece = h_pool.tile([P, PACK, FEATURES], BF16, name="h")
                    rows = PACK
                else:
                    piece = h_first.tile([P, PACK, K_PASS], BF16, name="h_half")
                    rows = ROWS_PER_BANK
                for j0 in range(0, PACK, rows):
                    nc.sync.dma_start(
                        out=piece[:, j0 : j0 + rows, :], in_=h_groups[i][:, j0 : j0 + rows, start : start + width]
                    )
                h[i].append(piece)

        for i in range(PREFETCH):
            load_frames(i)

        warm = consts.tile([P, 2], F32, name="warm")
        nc.vector.memset(warm[:], 0.0)
        nc.scalar.activation(out=warm[:, 1:2], in_=warm[:, 0:1], func=SIGMOID)

        ident_f32 = consts.tile([P, P], F32, name="ident_f32")
        make_identity(nc, ident_f32[:])
        ident_bf16 = consts.tile([P, P], BF16, name="ident_bf16")
        make_identity(nc, ident_bf16[:])

        w_words = consts.tile([P, FEATURE_PASSES, SLOTS], U32, name="w_words", align_bytes=64)
        nc.sync.dma_start(
            out=w_words[:].bitcast(I32),
            in_=Wr_words.rearrange("g p n t -> p g (n t)").bitcast(I32),
        )
        w_scales = consts.tile([P, FEATURE_PASSES, SLOTS], U8, name="w_scales", align_bytes=64)
        nc.vector.memset(w_scales[:].bitcast(I32), 0)
        for quad in range(P // QUADRANT):
            nc.sync.dma_start(
                out=w_scales[QUADRANT * quad : QUADRANT * quad + 4, :, :].bitcast(I32),
                in_=Wr_scales[:, 4 * quad : 4 * quad + 4, :].rearrange("g r n -> r g n").bitcast(I32),
            )

        bias_rows = consts.tile([P, P], BF16, name="bias_rows")
        nc.vector.memset(bias_rows[:], 0.0)
        nc.sync.dma_start(out=bias_rows[0:1, :], in_=br.unsqueeze(0))
        bias_ps = ps_one.tile([P, PACK, P], BF16, name="route_ps")
        nc.tensor.transpose(bias_ps[:, 0, :], bias_rows[:], ident_bf16[:])
        bias = consts.tile([P, 1], F32, name="bias")
        nc.vector.tensor_copy(out=bias[:], in_=bias_ps[:, 0, 0:1])

        def regroup(copy, i, start, stop):
            if i not in by_frame:
                by_frame[i] = frames.tile([P, FEATURES, PACK], BF16, name="by_frame", align_bytes=64)
            copy(
                out=by_frame[i][:, start:stop, :].rearrange("p (c r) j -> p c j r", r=RUN),
                in_=frames_of(i, start, stop).rearrange("p j (c r) -> p c j r", r=RUN),
            )

        def transpose_features(i, g):
            if g == 0:
                by_feature[i] = near.tile([P, FEATURE_PASSES, K_PASS, PACK], BF16, name="by_feature", align_bytes=64)
            for j0 in range(0, PACK, ROWS_PER_BANK):
                xt = xt_pool.tile([P, ROWS_PER_BANK, PAIR, P], F32, name="xt")
                for r in range(ROWS_PER_BANK):
                    words = frames_of(i, K_PASS * g, K_PASS * (g + 1))[:, j0 + r, :].bitcast(F32)
                    for u in range(PAIR):
                        nc.tensor.transpose(
                            xt[:, r, u, :],
                            words[:, u:PASS_WORDS:PAIR],
                            ident_f32[:],
                        )
                columns = by_feature[i][:, g, P * j0 : P * (j0 + ROWS_PER_BANK), :]
                nc.scalar.copy(
                    out=columns.rearrange("p n t -> p (n t)")
                    .bitcast(F32)
                    .rearrange("p (r n u) -> p r n u", r=ROWS_PER_BANK, u=PAIR),
                    in_=xt[:].rearrange("p r u n -> p r n u"),
                )

        def quantise_features(i):
            feature_codes[i] = near.tile([P, FEATURE_PASSES, K_PASS], U32, name="feature_codes", align_bytes=64)
            feature_scales[i] = near.tile([P, FEATURE_PASSES, K_PASS], U8, name="feature_scales", align_bytes=64)
            for g in range(FEATURE_PASSES):
                nc.vector.quantize_mx(
                    out=feature_codes[i][:, g, :].bitcast(FP8X4),
                    scales=feature_scales[i][:, g, :],
                    in_=by_feature[i][:, g, :, :].rearrange("p n t -> p (n t)"),
                )

        def route_logits(i):
            logits[i] = ps_one.tile([P, K_PASS], F32, name="logits")
            for g in range(FEATURE_PASSES):
                nc.tensor.matmul_mx(
                    out=logits[i][:],
                    lhsT=w_words[:, g, :].bitcast(FP8X4),
                    lhsT_scale=w_scales[:, g, :],
                    rhs=feature_codes[i][:, g, :].bitcast(FP8X4),
                    rhs_scale=feature_scales[i][:, g, :],
                    start=(g == 0),
                    stop=(g == FEATURE_PASSES - 1),
                )

        def route_sigmoid(i):
            route_t[i] = near.tile([P, K_PASS], BF16, name="route_t")
            nc.scalar.activation(
                out=route_t[i][:].rearrange("s (u p e) -> s u p e", u=PAIR, e=PAIR),
                in_=logits[i][:].rearrange("s (u e p) -> s u p e", u=PAIR, e=PAIR),
                func=SIGMOID,
                bias=bias[:],
                scale=1.0,
            )

        def transpose_route(i):
            route_ps = ps_one.tile([P, PAIR, P], F32, name="route_ps")
            words = route_t[i][:].bitcast(F32)
            for u in range(PAIR):
                nc.tensor.transpose(route_ps[:, u, :], words[:, P * u : P * (u + 1)], ident_f32[:])
            route_w[i] = near.tile([P, SLOTS, PACK], BF16, name="route_w", align_bytes=64)
            nc.scalar.copy(
                out=route_w[i][:].rearrange("p k j -> p (k j)").bitcast(F32).rearrange("p (k u) -> p k u", u=PAIR),
                in_=route_ps[:].rearrange("p u k -> p k u"),
            )

        def quantise_route(i):
            route_codes[i] = near.tile([P, SLOTS], U32, name="route_codes", align_bytes=64)
            route_scales[i] = near.tile([P, SLOTS], U8, name="route_scales", align_bytes=64)
            nc.vector.quantize_mx(
                out=route_codes[i][:].bitcast(FP8X4),
                scales=route_scales[i][:],
                in_=route_w[i][:].rearrange("p k j -> p (k j)"),
            )

        def quantise_frames(i):
            frame_codes[i] = far.tile([P, FEATURES], U32, name="frame_codes", align_bytes=64)
            frame_scales[i] = far.tile([P, FEATURES], U8, name="frame_scales", align_bytes=64)
            nc.vector.quantize_mx(
                out=frame_codes[i][:].bitcast(FP8X4),
                scales=frame_scales[i][:],
                in_=by_frame[i][:].rearrange("p d j -> p (d j)"),
            )

        def pool_frames(i):
            seq, c = divmod(i, GROUPS_PER_SEQ)
            for b in range(FEATURE_BANKS):
                if c == 0:
                    agg[b] = ps_one.tile([P, BANK], F32, name="agg%d" % b)
                nc.tensor.matmul_mx(
                    out=agg[b][:],
                    lhsT=route_codes[i][:].bitcast(FP8X4),
                    lhsT_scale=route_scales[i][:],
                    rhs=frame_codes[i][:, BANK * b : BANK * (b + 1)].bitcast(FP8X4),
                    rhs_scale=frame_scales[i][:, BANK * b : BANK * (b + 1)],
                    start=(c == 0),
                    stop=(c == GROUPS_PER_SEQ - 1),
                )

        def pool_round(i):
            return i + LAG_POOL + NEW_SEQ_LAG * (i // GROUPS_PER_SEQ)

        def empty_bank(seq, b, copy):
            result = near.tile([P, BANK], F32, name="result")
            copy(out=result[:], in_=agg[b][:])
            nc.sync.dma_start(out=out[seq, :, BANK * b : BANK * (b + 1)], in_=result[:])

        last = N_GROUPS - 1
        with tc.manual_schedule():
            for n in range(pool_round(last) + 2):
                finished = [k for k in range(SEQS) if pool_round(GROUPS_PER_SEQ * (k + 1) - 1) == n - 1]
                if live(n + PREFETCH):
                    load_frames(n + PREFETCH)
                if 0 < n < last:
                    regroup(nc.scalar.copy, n, VECTOR_COLS, FEATURES)
                if live(n):
                    transpose_features(n, 0)
                if live(n - LAG_LOGITS):
                    route_logits(n - LAG_LOGITS)
                if live(n):
                    transpose_features(n, 1)
                for seq in finished:
                    empty_bank(seq, 0, nc.scalar.copy)
                if live(n - LAG_LOGITS):
                    route_sigmoid(n - LAG_LOGITS)
                if live(n - LAG_ROUTE_T):
                    transpose_route(n - LAG_ROUTE_T)
                if n == last:
                    regroup(nc.scalar.copy, n, LAST_VECTOR_COLS, FEATURES)
                if live(n - LAG_QUANTISE):
                    quantise_features(n - LAG_QUANTISE)
                for seq in finished:
                    empty_bank(seq, 1, nc.vector.tensor_copy)
                if live(n - LAG_ROUTE_Q):
                    quantise_route(n - LAG_ROUTE_Q)
                if live(n - LAG_FRAMES_Q):
                    quantise_frames(n - LAG_FRAMES_Q)
                if n == 0:
                    for start in range(0, FEATURES, K_PASS):
                        regroup(nc.vector.tensor_copy, n, start, start + K_PASS)
                elif n < last:
                    regroup(nc.vector.tensor_copy, n, 0, VECTOR_COLS)
                elif n == last + 1:
                    regroup(nc.vector.tensor_copy, last, 0, LAST_VECTOR_COLS)
                for i in range(N_GROUPS):
                    if pool_round(i) == n:
                        pool_frames(i)
